import numpy as np
import ml_dtypes

BF16 = ml_dtypes.bfloat16


def bf(x):
    return np.asarray(x, np.float32).astype(BF16)


def f32(x):
    return np.asarray(x, np.float32)


def f64(x):
    return np.asarray(x).astype(np.float64)


def striped(idx):
    return np.tile(idx.reshape(-1, 16).T, (8, 1))


K, C, S, N = 512, 128, 2048, 1024
DENS = 1.0 / 64.0
SIG_MU, SIG, SIG_BASE = 0.25, 0.2, 0.12


def lift(sp, axis):
    t = np.sqrt(1.0 + np.sum(f64(sp) ** 2, axis=axis, keepdims=True))
    return f32(np.concatenate([t, f64(sp)], axis=axis))


def setup_inputs():
    mu = SIG_MU * np.random.standard_normal((1, C - 1))
    h = lift(f32(mu + SIG * np.random.standard_normal((K, C - 1))), 1)
    mask = (np.random.random_sample((K, N)) < DENS).astype(np.float64)
    mask[np.arange(N) % K, np.arange(N)] = 1.0
    adj_t = bf(mask / np.sum(mask, axis=0, keepdims=True))
    base = lift(f32(SIG_BASE * np.random.standard_normal((C - 1, S))), 0)
    return {"h": h, "adj_t": adj_t, "base": base, "offs": striped(np.random.permutation(S)[:N])}


def reference(h, adj_t, base, offs):
    idx = offs[:16].T.reshape(-1)
    m = f64(h).T @ f64(adj_t)
    q = -m[:1] ** 2 + np.sum(m[1:] ** 2, axis=0, keepdims=True)
    out = f64(base).copy()
    out[:, idx] = m * (1.0 / np.sqrt(np.abs(q)))
    return out

@@ -1,0 +1,88 @@
+import concourse.mybir as mybir
+
+F32 = mybir.dt.float32
+BF16 = mybir.dt.bfloat16
+U16 = mybir.dt.uint16
+MULT = mybir.AluOpType.mult
+SQUARE = mybir.ActivationFunctionType.Square
+ABS_RSQRT = mybir.ActivationFunctionType.Abs_reciprocal_sqrt
+
+P = 128
+SOURCES = 512
+TARGETS = 1024
+STORE = 2048
+K_BLOCKS = SOURCES // P
+PIECE = 512
+PIECES = TARGETS // PIECE
+OFFS_COLS = PIECE // 16
+HALVES = 2
+HALF = PIECE // HALVES
+WARM_MATMULS = 12
+
+FLOPS = 2 * SOURCES * P * TARGETS + 4 * P * TARGETS
+
+
+def tile_fulllorentzgraphneuralnetwork_kernel(tc, h, adj_t, base, offs, out):
+    nc = tc.nc
+    with (
+        tc.tile_pool(name="held", bufs=1) as held,
+        tc.psum_pool(name="psum", bufs=1) as psum,
+    ):
+        h_f32 = held.tile([P, K_BLOCKS, P], F32, name="h_f32")
+        nc.sync.dma_start(h_f32[:], h.rearrange("(p k) c -> p k c", k=K_BLOCKS))
+
+        adj_blocks = adj_t.rearrange("(p k) j -> p k j", k=K_BLOCKS)
+        adj = [[held.tile([P, PIECE], BF16, name=f"adj{piece}_{k}") for k in range(K_BLOCKS)] for piece in range(PIECES)]
+        offsets = held.tile([P, TARGETS // 16], U16, name="offsets")
+        window = held.tile([P, STORE], F32, name="window")
+        for piece in range(PIECES):
+            for k in range(K_BLOCKS):
+                nc.sync.dma_start(adj[piece][k][:], adj_blocks[:, k, piece * PIECE : (piece + 1) * PIECE])
+            if piece == 0:
+                nc.sync.dma_start(offsets[:], offs)
+                nc.sync.dma_start(window[:], base)
+
+        minkowski = held.tile([P, P], BF16, name="minkowski")
+        nc.vector.memset(minkowski[:], 1.0)
+        nc.vector.memset(minkowski[0:1, :], -1.0)
+
+        warm_psum = psum.tile([P, P], F32, name="warm_psum")
+        for repeat in range(WARM_MATMULS):
+            nc.tensor.matmul(warm_psum[:], minkowski[:], minkowski[:], start=True, stop=True)
+
+        scratch = held.tile([P, 1], F32, name="scratch")
+        nc.vector.memset(scratch[:], 1.0)
+        nc.scalar.activation(scratch[:], scratch[:], ABS_RSQRT)
+
+        h_bf16 = [held.tile([P, P], BF16, name=f"h_bf16_{k}") for k in range(K_BLOCKS)]
+        for k in range(K_BLOCKS):
+            nc.vector.tensor_copy(h_bf16[k][:], h_f32[:, k, :])
+
+        for piece in range(PIECES):
+            m_sbuf = held.tile([P, PIECE], F32, name=f"m_sbuf{piece}")
+            inv_norm = held.tile([P, PIECE], F32, name=f"inv_norm{piece}")
+            for half in range(HALVES):
+                columns = slice(half * HALF, (half + 1) * HALF)
+
+                m_psum = psum.tile([P, HALF], F32, name=f"m_psum{piece}_{half}")
+                for k in range(K_BLOCKS):
+                    nc.tensor.matmul(
+                        m_psum[:], h_bf16[k][:], adj[piece][k][:, columns], start=(k == 0), stop=(k == K_BLOCKS - 1)
+                    )
+
+                squares = held.tile([P, HALF], BF16, name=f"squares{piece}_{half}")
+                nc.scalar.activation(squares[:], m_psum[:], SQUARE)
+                q_psum = psum.tile([P, HALF], F32, name=f"q_psum{half}")
+                nc.tensor.matmul(q_psum[:], minkowski[:], squares[:], start=True, stop=True)
+
+                if piece == 0:
+                    nc.vector.tensor_copy(m_sbuf[:, columns], m_psum[:])
+                else:
+                    nc.scalar.copy(m_sbuf[:, columns], m_psum[:])
+
+                nc.scalar.activation(inv_norm[:, columns], q_psum[:], ABS_RSQRT)
+
+            piece_offsets = offsets[:, piece * OFFS_COLS : (piece + 1) * OFFS_COLS]
+            nc.vector.tensor_tensor(window[:].indirect(piece_offsets), m_sbuf[:], inv_norm[:], MULT)
+
+        nc.sync.dma_start(out, window[:])

@@ -18,6 +18,7 @@ OFFS_COLS = PIECE // 16
 HALVES = 2
 HALF = PIECE // HALVES
 WARM_MATMULS = 12
+KEEP_WARM_MATMULS = 4
 
 FLOPS = 2 * SOURCES * P * TARGETS + 4 * P * TARGETS
 
@@ -46,9 +47,9 @@ def tile_fulllorentzgraphneuralnetwork_kernel(tc, h, adj_t, base, offs, out):
         nc.vector.memset(minkowski[:], 1.0)
         nc.vector.memset(minkowski[0:1, :], -1.0)
 
-        warm_psum = psum.tile([P, P], F32, name="warm_psum")
+        warm_psum = psum.tile([P, HALF], F32, name="warm_psum")
         for repeat in range(WARM_MATMULS):
-            nc.tensor.matmul(warm_psum[:], minkowski[:], minkowski[:], start=True, stop=True)
+            nc.tensor.matmul(warm_psum[:, :P], minkowski[:], minkowski[:], start=True, stop=True)
 
         scratch = held.tile([P, 1], F32, name="scratch")
         nc.vector.memset(scratch[:], 1.0)
@@ -81,6 +82,10 @@ def tile_fulllorentzgraphneuralnetwork_kernel(tc, h, adj_t, base, offs, out):
                     nc.scalar.copy(m_sbuf[:, columns], m_psum[:])
 
                 nc.scalar.activation(inv_norm[:, columns], q_psum[:], ABS_RSQRT)
+
+            if piece == 0:
+                for repeat in range(KEEP_WARM_MATMULS):
+                    nc.tensor.matmul(warm_psum[:], minkowski[:], squares[:], start=True, stop=True)
 
             piece_offsets = offsets[:, piece * OFFS_COLS : (piece + 1) * OFFS_COLS]
             nc.vector.tensor_tensor(window[:].indirect(piece_offsets), m_sbuf[:], inv_norm[:], MULT)

@@ -17,8 +17,9 @@ PIECES = TARGETS // PIECE
 OFFS_COLS = PIECE // 16
 HALVES = 2
 HALF = PIECE // HALVES
+PART = 128
 WARM_MATMULS = 12
-KEEP_WARM_MATMULS = 4
+KEEP_WARM_MATMULS = 8
 
 FLOPS = 2 * SOURCES * P * TARGETS + 4 * P * TARGETS
 
@@ -47,9 +48,9 @@ def tile_fulllorentzgraphneuralnetwork_kernel(tc, h, adj_t, base, offs, out):
         nc.vector.memset(minkowski[:], 1.0)
         nc.vector.memset(minkowski[0:1, :], -1.0)
 
-        warm_psum = psum.tile([P, HALF], F32, name="warm_psum")
+        warm_psum = psum.tile([P, P], F32, name="warm_psum")
         for repeat in range(WARM_MATMULS):
-            nc.tensor.matmul(warm_psum[:, :P], minkowski[:], minkowski[:], start=True, stop=True)
+            nc.tensor.matmul(warm_psum[:], minkowski[:], minkowski[:], start=True, stop=True)
 
         scratch = held.tile([P, 1], F32, name="scratch")
         nc.vector.memset(scratch[:], 1.0)
@@ -59,35 +60,42 @@ def tile_fulllorentzgraphneuralnetwork_kernel(tc, h, adj_t, base, offs, out):
         for k in range(K_BLOCKS):
             nc.vector.tensor_copy(h_bf16[k][:], h_f32[:, k, :])
 
-        for piece in range(PIECES):
-            m_sbuf = held.tile([P, PIECE], F32, name=f"m_sbuf{piece}")
-            inv_norm = held.tile([P, PIECE], F32, name=f"inv_norm{piece}")
-            for half in range(HALVES):
-                columns = slice(half * HALF, (half + 1) * HALF)
+        m_sbuf = [held.tile([P, PIECE], F32, name=f"m_sbuf{piece}") for piece in range(PIECES)]
+        inv_norm = [held.tile([P, PIECE], F32, name=f"inv_norm{piece}") for piece in range(PIECES)]
 
-                m_psum = psum.tile([P, HALF], F32, name=f"m_psum{piece}_{half}")
-                for k in range(K_BLOCKS):
-                    nc.tensor.matmul(
-                        m_psum[:], h_bf16[k][:], adj[piece][k][:, columns], start=(k == 0), stop=(k == K_BLOCKS - 1)
-                    )
-
-                squares = held.tile([P, HALF], BF16, name=f"squares{piece}_{half}")
-                nc.scalar.activation(squares[:], m_psum[:], SQUARE)
-                q_psum = psum.tile([P, HALF], F32, name=f"q_psum{half}")
+        for half in range(HALVES):
+            half_columns = slice(half * HALF, (half + 1) * HALF)
+            m_psum = psum.tile([P, HALF], F32, name=f"m_psum0_{half}")
+            for k in range(K_BLOCKS):
+                nc.tensor.matmul(
+                    m_psum[:], h_bf16[k][:], adj[0][k][:, half_columns], start=(k == 0), stop=(k == K_BLOCKS - 1)
+                )
+            for part in range(HALF // PART):
+                in_half = slice(part * PART, (part + 1) * PART)
+                squares = held.tile([P, PART], BF16, name=f"squares0_{half}_{part}")
+                nc.scalar.activation(squares[:], m_psum[:, in_half], SQUARE)
+                q_psum = psum.tile([P, PART], F32, name=f"q_psum0_{part}")
                 nc.tensor.matmul(q_psum[:], minkowski[:], squares[:], start=True, stop=True)
+                in_piece = slice(half * HALF + part * PART, half * HALF + (part + 1) * PART)
+                nc.scalar.activation(inv_norm[0][:, in_piece], q_psum[:], ABS_RSQRT)
+            nc.vector.tensor_copy(m_sbuf[0][:, half_columns], m_psum[:])
 
-                if piece == 0:
-                    nc.vector.tensor_copy(m_sbuf[:, columns], m_psum[:])
-                else:
-                    nc.scalar.copy(m_sbuf[:, columns], m_psum[:])
+        for repeat in range(KEEP_WARM_MATMULS):
+            nc.tensor.matmul(warm_psum[:], minkowski[:], squares[:], start=True, stop=True)
 
-                nc.scalar.activation(inv_norm[:, columns], q_psum[:], ABS_RSQRT)
+        nc.vector.tensor_tensor(window[:].indirect(offsets[:, :OFFS_COLS]), m_sbuf[0][:], inv_norm[0][:], MULT)
 
-            if piece == 0:
-                for repeat in range(KEEP_WARM_MATMULS):
-                    nc.tensor.matmul(warm_psum[:], minkowski[:], squares[:], start=True, stop=True)
-
-            piece_offsets = offsets[:, piece * OFFS_COLS : (piece + 1) * OFFS_COLS]
-            nc.vector.tensor_tensor(window[:].indirect(piece_offsets), m_sbuf[:], inv_norm[:], MULT)
+        m_psum = psum.tile([P, PIECE], F32, name="m_psum1")
+        for k in range(K_BLOCKS):
+            nc.tensor.matmul(m_psum[:], h_bf16[k][:], adj[1][k][:], start=(k == 0), stop=(k == K_BLOCKS - 1))
+        q_psum = psum.tile([P, PIECE], F32, name="q_psum1")
+        for half in range(HALVES):
+            half_columns = slice(half * HALF, (half + 1) * HALF)
+            squares = held.tile([P, HALF], BF16, name=f"squares1_{half}")
+            nc.scalar.activation(squares[:], m_psum[:, half_columns], SQUARE)
+            nc.tensor.matmul(q_psum[:, half_columns], minkowski[:], squares[:], start=True, stop=True)
+        nc.scalar.copy(m_sbuf[1][:], m_psum[:])
+        nc.scalar.activation(inv_norm[1][:], q_psum[:], ABS_RSQRT)
+        nc.vector.tensor_tensor(window[:].indirect(offsets[:, OFFS_COLS:]), m_sbuf[1][:], inv_norm[1][:], MULT)
 
         nc.sync.dma_start(out, window[:])

@@ -85,17 +85,19 @@ def tile_fulllorentzgraphneuralnetwork_kernel(tc, h, adj_t, base, offs, out):
 
         nc.vector.tensor_tensor(window[:].indirect(offsets[:, :OFFS_COLS]), m_sbuf[0][:], inv_norm[0][:], MULT)
 
-        m_psum = psum.tile([P, PIECE], F32, name="m_psum1")
-        for k in range(K_BLOCKS):
-            nc.tensor.matmul(m_psum[:], h_bf16[k][:], adj[1][k][:], start=(k == 0), stop=(k == K_BLOCKS - 1))
-        q_psum = psum.tile([P, PIECE], F32, name="q_psum1")
         for half in range(HALVES):
             half_columns = slice(half * HALF, (half + 1) * HALF)
+            m_psum = psum.tile([P, HALF], F32, name=f"m_psum1_{half}")
+            for k in range(K_BLOCKS):
+                nc.tensor.matmul(
+                    m_psum[:], h_bf16[k][:], adj[1][k][:, half_columns], start=(k == 0), stop=(k == K_BLOCKS - 1)
+                )
             squares = held.tile([P, HALF], BF16, name=f"squares1_{half}")
-            nc.scalar.activation(squares[:], m_psum[:, half_columns], SQUARE)
-            nc.tensor.matmul(q_psum[:, half_columns], minkowski[:], squares[:], start=True, stop=True)
-        nc.scalar.copy(m_sbuf[1][:], m_psum[:])
-        nc.scalar.activation(inv_norm[1][:], q_psum[:], ABS_RSQRT)
+            nc.scalar.activation(squares[:], m_psum[:], SQUARE)
+            q_psum = psum.tile([P, HALF], F32, name=f"q_psum1_{half}", tag=f"q_psum0_{half}")
+            nc.tensor.matmul(q_psum[:], minkowski[:], squares[:], start=True, stop=True)
+            nc.scalar.copy(m_sbuf[1][:, half_columns], m_psum[:])
+            nc.scalar.activation(inv_norm[1][:, half_columns], q_psum[:], ABS_RSQRT)
         nc.vector.tensor_tensor(window[:].indirect(offsets[:, OFFS_COLS:]), m_sbuf[1][:], inv_norm[1][:], MULT)
 
         nc.sync.dma_start(out, window[:])

@@ -34,12 +34,16 @@ def tile_fulllorentzgraphneuralnetwork_kernel(tc, h, adj_t, base, offs, out):
         nc.sync.dma_start(h_f32[:], h.rearrange("(p k) c -> p k c", k=K_BLOCKS))
 
         adj_blocks = adj_t.rearrange("(p k) j -> p k j", k=K_BLOCKS)
-        adj = [[held.tile([P, PIECE], BF16, name=f"adj{piece}_{k}") for k in range(K_BLOCKS)] for piece in range(PIECES)]
+        adj = [
+            [held.tile([P, 2, PIECE], BF16, name=f"adj{piece}_{pair}") for pair in range(K_BLOCKS // 2)]
+            for piece in range(PIECES)
+        ]
         offsets = held.tile([P, TARGETS // 16], U16, name="offsets")
         window = held.tile([P, STORE], F32, name="window")
         for piece in range(PIECES):
-            for k in range(K_BLOCKS):
-                nc.sync.dma_start(adj[piece][k][:], adj_blocks[:, k, piece * PIECE : (piece + 1) * PIECE])
+            for pair in range(K_BLOCKS // 2):
+                blocks = adj_blocks[:, 2 * pair : 2 * pair + 2, piece * PIECE : (piece + 1) * PIECE]
+                nc.sync.dma_start(adj[piece][pair][:], blocks)
             if piece == 0:
                 nc.sync.dma_start(offsets[:], offs)
                 nc.sync.dma_start(window[:], base)
@@ -68,13 +72,13 @@ def tile_fulllorentzgraphneuralnetwork_kernel(tc, h, adj_t, base, offs, out):
             m_psum = psum.tile([P, HALF], F32, name=f"m_psum0_{half}")
             for k in range(K_BLOCKS):
                 nc.tensor.matmul(
-                    m_psum[:], h_bf16[k][:], adj[0][k][:, half_columns], start=(k == 0), stop=(k == K_BLOCKS - 1)
+                    m_psum[:], h_bf16[k][:], adj[0][k // 2][:, k % 2, half_columns], start=(k == 0), stop=(k == K_BLOCKS - 1)
                 )
             for part in range(HALF // PART):
                 in_half = slice(part * PART, (part + 1) * PART)
                 squares = held.tile([P, PART], BF16, name=f"squares0_{half}_{part}")
                 nc.scalar.activation(squares[:], m_psum[:, in_half], SQUARE)
-                q_psum = psum.tile([P, PART], F32, name=f"q_psum0_{part}")
+                q_psum = psum.tile([P, PART], F32, name=f"q_psum0_{half}_{part}")
                 nc.tensor.matmul(q_psum[:], minkowski[:], squares[:], start=True, stop=True)
                 in_piece = slice(half * HALF + part * PART, half * HALF + (part + 1) * PART)
                 nc.scalar.activation(inv_norm[0][:, in_piece], q_psum[:], ABS_RSQRT)
@@ -87,14 +91,14 @@ def tile_fulllorentzgraphneuralnetwork_kernel(tc, h, adj_t, base, offs, out):
 
         for half in range(HALVES):
             half_columns = slice(half * HALF, (half + 1) * HALF)
-            m_psum = psum.tile([P, HALF], F32, name=f"m_psum1_{half}")
+            m_psum = psum.tile([P, HALF], F32, name=f"m_psum1_{half}", tag=f"m_psum0_{half}")
             for k in range(K_BLOCKS):
                 nc.tensor.matmul(
-                    m_psum[:], h_bf16[k][:], adj[1][k][:, half_columns], start=(k == 0), stop=(k == K_BLOCKS - 1)
+                    m_psum[:], h_bf16[k][:], adj[1][k // 2][:, k % 2, half_columns], start=(k == 0), stop=(k == K_BLOCKS - 1)
                 )
             squares = held.tile([P, HALF], BF16, name=f"squares1_{half}")
             nc.scalar.activation(squares[:], m_psum[:], SQUARE)
-            q_psum = psum.tile([P, HALF], F32, name=f"q_psum1_{half}", tag=f"q_psum0_{half}")
+            q_psum = psum.tile([P, HALF], F32, name=f"q_psum1_{half}", tag=f"q_psum0_{half}_0")
             nc.tensor.matmul(q_psum[:], minkowski[:], squares[:], start=True, stop=True)
             nc.scalar.copy(m_sbuf[1][:, half_columns], m_psum[:])
             nc.scalar.activation(inv_norm[1][:, half_columns], q_psum[:], ABS_RSQRT)

@@ -34,19 +34,18 @@ def tile_fulllorentzgraphneuralnetwork_kernel(tc, h, adj_t, base, offs, out):
         nc.sync.dma_start(h_f32[:], h.rearrange("(p k) c -> p k c", k=K_BLOCKS))
 
         adj_blocks = adj_t.rearrange("(p k) j -> p k j", k=K_BLOCKS)
-        adj = [
-            [held.tile([P, 2, PIECE], BF16, name=f"adj{piece}_{pair}") for pair in range(K_BLOCKS // 2)]
-            for piece in range(PIECES)
-        ]
         offsets = held.tile([P, TARGETS // 16], U16, name="offsets")
         window = held.tile([P, STORE], F32, name="window")
-        for piece in range(PIECES):
-            for pair in range(K_BLOCKS // 2):
-                blocks = adj_blocks[:, 2 * pair : 2 * pair + 2, piece * PIECE : (piece + 1) * PIECE]
-                nc.sync.dma_start(adj[piece][pair][:], blocks)
-            if piece == 0:
-                nc.sync.dma_start(offsets[:], offs)
-                nc.sync.dma_start(window[:], base)
+
+        adj_first = [held.tile([P, 2, PIECE], BF16, name=f"adj_first{pair}") for pair in range(K_BLOCKS // 2)]
+        for pair in range(K_BLOCKS // 2):
+            nc.sync.dma_start(adj_first[pair][:], adj_blocks[:, 2 * pair : 2 * pair + 2, :PIECE])
+        nc.sync.dma_start(offsets[:], offs)
+        nc.sync.dma_start(window[:], base)
+        adj_second = [held.tile([P, K_BLOCKS, HALF], BF16, name=f"adj_second{half}") for half in range(HALVES)]
+        for half in range(HALVES):
+            start = PIECE + half * HALF
+            nc.sync.dma_start(adj_second[half][:], adj_blocks[:, :, start : start + HALF])
 
         minkowski = held.tile([P, P], BF16, name="minkowski")
         nc.vector.memset(minkowski[:], 1.0)
@@ -72,7 +71,7 @@ def tile_fulllorentzgraphneuralnetwork_kernel(tc, h, adj_t, base, offs, out):
             m_psum = psum.tile([P, HALF], F32, name=f"m_psum0_{half}")
             for k in range(K_BLOCKS):
                 nc.tensor.matmul(
-                    m_psum[:], h_bf16[k][:], adj[0][k // 2][:, k % 2, half_columns], start=(k == 0), stop=(k == K_BLOCKS - 1)
+                    m_psum[:], h_bf16[k][:], adj_first[k // 2][:, k % 2, half_columns], start=(k == 0), stop=(k == K_BLOCKS - 1)
                 )
             for part in range(HALF // PART):
                 in_half = slice(part * PART, (part + 1) * PART)
@@ -94,7 +93,7 @@ def tile_fulllorentzgraphneuralnetwork_kernel(tc, h, adj_t, base, offs, out):
             m_psum = psum.tile([P, HALF], F32, name=f"m_psum1_{half}", tag=f"m_psum0_{half}")
             for k in range(K_BLOCKS):
                 nc.tensor.matmul(
-                    m_psum[:], h_bf16[k][:], adj[1][k // 2][:, k % 2, half_columns], start=(k == 0), stop=(k == K_BLOCKS - 1)
+                    m_psum[:], h_bf16[k][:], adj_second[half][:, k, :], start=(k == 0), stop=(k == K_BLOCKS - 1)
                 )
             squares = held.tile([P, HALF], BF16, name=f"squares1_{half}")
             nc.scalar.activation(squares[:], m_psum[:], SQUARE)

@@ -66,41 +66,33 @@ def tile_fulllorentzgraphneuralnetwork_kernel(tc, h, adj_t, base, offs, out):
         m_sbuf = [held.tile([P, PIECE], F32, name=f"m_sbuf{piece}") for piece in range(PIECES)]
         inv_norm = [held.tile([P, PIECE], F32, name=f"inv_norm{piece}") for piece in range(PIECES)]
 
-        for half in range(HALVES):
-            half_columns = slice(half * HALF, (half + 1) * HALF)
-            m_psum = psum.tile([P, HALF], F32, name=f"m_psum0_{half}")
-            for k in range(K_BLOCKS):
-                nc.tensor.matmul(
-                    m_psum[:], h_bf16[k][:], adj_first[k // 2][:, k % 2, half_columns], start=(k == 0), stop=(k == K_BLOCKS - 1)
-                )
-            for part in range(HALF // PART):
-                in_half = slice(part * PART, (part + 1) * PART)
-                squares = held.tile([P, PART], BF16, name=f"squares0_{half}_{part}")
-                nc.scalar.activation(squares[:], m_psum[:, in_half], SQUARE)
-                q_psum = psum.tile([P, PART], F32, name=f"q_psum0_{half}_{part}")
-                nc.tensor.matmul(q_psum[:], minkowski[:], squares[:], start=True, stop=True)
-                in_piece = slice(half * HALF + part * PART, half * HALF + (part + 1) * PART)
-                nc.scalar.activation(inv_norm[0][:, in_piece], q_psum[:], ABS_RSQRT)
-            nc.vector.tensor_copy(m_sbuf[0][:, half_columns], m_psum[:])
+        for piece in range(PIECES):
+            for half in range(HALVES):
+                half_columns = slice(half * HALF, (half + 1) * HALF)
+                m_psum = psum.tile([P, HALF], F32, name=f"m_psum{piece}_{half}", tag=f"m_psum{half}")
+                for k in range(K_BLOCKS):
+                    adj = adj_first[k // 2][:, k % 2, half_columns] if piece == 0 else adj_second[half][:, k, :]
+                    nc.tensor.matmul(m_psum[:], h_bf16[k][:], adj, start=(k == 0), stop=(k == K_BLOCKS - 1))
 
-        for repeat in range(KEEP_WARM_MATMULS):
-            nc.tensor.matmul(warm_psum[:], minkowski[:], squares[:], start=True, stop=True)
+                for part in range(HALF // PART):
+                    in_half = slice(part * PART, (part + 1) * PART)
+                    squares = held.tile([P, PART], BF16, name=f"squares{piece}_{half}_{part}")
+                    nc.scalar.activation(squares[:], m_psum[:, in_half], SQUARE)
+                    q_psum = psum.tile([P, PART], F32, name=f"q_psum{piece}_{half}_{part}", tag=f"q_psum{half}_{part}")
+                    nc.tensor.matmul(q_psum[:], minkowski[:], squares[:], start=True, stop=True)
+                    in_piece = slice(half * HALF + part * PART, half * HALF + (part + 1) * PART)
+                    nc.scalar.activation(inv_norm[piece][:, in_piece], q_psum[:], ABS_RSQRT)
 
-        nc.vector.tensor_tensor(window[:].indirect(offsets[:, :OFFS_COLS]), m_sbuf[0][:], inv_norm[0][:], MULT)
+                if piece == 0:
+                    nc.vector.tensor_copy(m_sbuf[piece][:, half_columns], m_psum[:])
+                else:
+                    nc.scalar.copy(m_sbuf[piece][:, half_columns], m_psum[:])
 
-        for half in range(HALVES):
-            half_columns = slice(half * HALF, (half + 1) * HALF)
-            m_psum = psum.tile([P, HALF], F32, name=f"m_psum1_{half}", tag=f"m_psum0_{half}")
-            for k in range(K_BLOCKS):
-                nc.tensor.matmul(
-                    m_psum[:], h_bf16[k][:], adj_second[half][:, k, :], start=(k == 0), stop=(k == K_BLOCKS - 1)
-                )
-            squares = held.tile([P, HALF], BF16, name=f"squares1_{half}")
-            nc.scalar.activation(squares[:], m_psum[:], SQUARE)
-            q_psum = psum.tile([P, HALF], F32, name=f"q_psum1_{half}", tag=f"q_psum0_{half}_0")
-            nc.tensor.matmul(q_psum[:], minkowski[:], squares[:], start=True, stop=True)
-            nc.scalar.copy(m_sbuf[1][:, half_columns], m_psum[:])
-            nc.scalar.activation(inv_norm[1][:, half_columns], q_psum[:], ABS_RSQRT)
-        nc.vector.tensor_tensor(window[:].indirect(offsets[:, OFFS_COLS:]), m_sbuf[1][:], inv_norm[1][:], MULT)
+            if piece == 0:
+                for repeat in range(KEEP_WARM_MATMULS):
+                    nc.tensor.matmul(warm_psum[:], minkowski[:], squares[:], start=True, stop=True)
+
+            piece_offsets = offsets[:, piece * OFFS_COLS : (piece + 1) * OFFS_COLS]
+            nc.vector.tensor_tensor(window[:].indirect(piece_offsets), m_sbuf[piece][:], inv_norm[piece][:], MULT)
 
         nc.sync.dma_start(out, window[:])

import concourse.mybir as mybir

F32 = mybir.dt.float32
BF16 = mybir.dt.bfloat16
U16 = mybir.dt.uint16
MULT = mybir.AluOpType.mult
SQUARE = mybir.ActivationFunctionType.Square
ABS_RSQRT = mybir.ActivationFunctionType.Abs_reciprocal_sqrt

P = 128
SOURCES = 512
TARGETS = 1024
STORE = 2048
K_BLOCKS = SOURCES // P
PIECE = 512
PIECES = TARGETS // PIECE
OFFS_COLS = PIECE // 16
HALVES = 2
HALF = PIECE // HALVES
PART = 128
WARM_MATMULS = 12
KEEP_WARM_MATMULS = 8

FLOPS = 2 * SOURCES * P * TARGETS + 4 * P * TARGETS


def tile_fulllorentzgraphneuralnetwork_kernel(tc, h, adj_t, base, offs, out):
    nc = tc.nc
    with (
        tc.tile_pool(name="held", bufs=1) as held,
        tc.psum_pool(name="psum", bufs=1) as psum,
    ):
        h_f32 = held.tile([P, K_BLOCKS, P], F32, name="h_f32")
        nc.sync.dma_start(h_f32[:], h.rearrange("(p k) c -> p k c", k=K_BLOCKS))

        adj_blocks = adj_t.rearrange("(p k) j -> p k j", k=K_BLOCKS)
        offsets = held.tile([P, TARGETS // 16], U16, name="offsets")
        window = held.tile([P, STORE], F32, name="window")

        adj_first = [held.tile([P, 2, PIECE], BF16, name=f"adj_first{pair}") for pair in range(K_BLOCKS // 2)]
        for pair in range(K_BLOCKS // 2):
            nc.sync.dma_start(adj_first[pair][:], adj_blocks[:, 2 * pair : 2 * pair + 2, :PIECE])
        nc.sync.dma_start(offsets[:], offs)
        nc.sync.dma_start(window[:], base)
        adj_second = [held.tile([P, K_BLOCKS, HALF], BF16, name=f"adj_second{half}") for half in range(HALVES)]
        for half in range(HALVES):
            start = PIECE + half * HALF
            nc.sync.dma_start(adj_second[half][:], adj_blocks[:, :, start : start + HALF])

        minkowski = held.tile([P, P], BF16, name="minkowski")
        nc.vector.memset(minkowski[:], 1.0)
        nc.vector.memset(minkowski[0:1, :], -1.0)

        warm_psum = psum.tile([P, P], F32, name="warm_psum")
        for repeat in range(WARM_MATMULS):
            nc.tensor.matmul(warm_psum[:], minkowski[:], minkowski[:], start=True, stop=True)

        scratch = held.tile([P, 1], F32, name="scratch")
        nc.vector.memset(scratch[:], 1.0)
        nc.scalar.activation(scratch[:], scratch[:], ABS_RSQRT)

        h_bf16 = [held.tile([P, P], BF16, name=f"h_bf16_{k}") for k in range(K_BLOCKS)]
        for k in range(K_BLOCKS):
            nc.vector.tensor_copy(h_bf16[k][:], h_f32[:, k, :])

        m_sbuf = [held.tile([P, PIECE], F32, name=f"m_sbuf{piece}") for piece in range(PIECES)]
        inv_norm = [held.tile([P, PIECE], F32, name=f"inv_norm{piece}") for piece in range(PIECES)]

        for piece in range(PIECES):
            for half in range(HALVES):
                half_columns = slice(half * HALF, (half + 1) * HALF)
                m_psum = psum.tile([P, HALF], F32, name=f"m_psum{piece}_{half}", tag=f"m_psum{half}")
                for k in range(K_BLOCKS):
                    adj = adj_first[k // 2][:, k % 2, half_columns] if piece == 0 else adj_second[half][:, k, :]
                    nc.tensor.matmul(m_psum[:], h_bf16[k][:], adj, start=(k == 0), stop=(k == K_BLOCKS - 1))

                for part in range(HALF // PART):
                    in_half = slice(part * PART, (part + 1) * PART)
                    squares = held.tile([P, PART], BF16, name=f"squares{piece}_{half}_{part}")
                    nc.scalar.activation(squares[:], m_psum[:, in_half], SQUARE)
                    q_psum = psum.tile([P, PART], F32, name=f"q_psum{piece}_{half}_{part}", tag=f"q_psum{half}_{part}")
                    nc.tensor.matmul(q_psum[:], minkowski[:], squares[:], start=True, stop=True)
                    in_piece = slice(half * HALF + part * PART, half * HALF + (part + 1) * PART)
                    nc.scalar.activation(inv_norm[piece][:, in_piece], q_psum[:], ABS_RSQRT)

                if piece == 0:
                    nc.vector.tensor_copy(m_sbuf[piece][:, half_columns], m_psum[:])
                else:
                    nc.scalar.copy(m_sbuf[piece][:, half_columns], m_psum[:])

            if piece == 0:
                for repeat in range(KEEP_WARM_MATMULS):
                    nc.tensor.matmul(warm_psum[:], minkowski[:], squares[:], start=True, stop=True)

            piece_offsets = offsets[:, piece * OFFS_COLS : (piece + 1) * OFFS_COLS]
            nc.vector.tensor_tensor(window[:].indirect(piece_offsets), m_sbuf[piece][:], inv_norm[piece][:], MULT)

        nc.sync.dma_start(out, window[:])
